import numpy as np
import ml_dtypes


def mxq(x, axis, fmt="e4m3"):
    dtype, down = {"e4m3": (ml_dtypes.float8_e4m3fn, 7), "e5m2": (ml_dtypes.float8_e5m2, 14)}[fmt]
    v = np.moveaxis(np.asarray(x, np.float32).astype(ml_dtypes.bfloat16).astype(np.float64), axis, -1)
    blocks = v.reshape(v.shape[:-1] + (-1, 32))
    amax = np.abs(blocks).max(-1, keepdims=True)
    byte = np.maximum(np.where(amax > 0, np.frexp(amax)[1] - 1 + 127, 0) - down, 1)
    scale = np.exp2(byte - 127.0)
    codes = (blocks / scale).astype(np.float32).astype(dtype).astype(np.float64)
    return np.moveaxis((codes * scale).reshape(v.shape), -1, axis)


WIDE = False


def mx_kscale(k):
    if not WIDE:
        return np.ones(k)
    levels = np.array([10, -10, 5, -5, 0])
    a = np.random.permutation(np.resize(levels, k // 512 * 4)).reshape(k // 512, 4)
    idx = np.arange(k)
    return np.exp2(a[idx // 512, idx % 128 // 32])


BF16 = ml_dtypes.bfloat16


def bf(x):
    return np.asarray(x, np.float32).astype(BF16)


def f64(x):
    return np.asarray(x).astype(np.float64)


B, N, DIN, H, EMB, CHEB = 16, 512, 384, 128, 10, 3
C = DIN + H
KC = CHEB * C


def draw_supports():
    emb = f64(bf(np.random.standard_normal((N, EMB))))
    l = np.maximum((emb[:, None, :] * emb[None, :, :]).sum(-1), 0.0)
    e = np.exp(l - l.max(1, keepdims=True))
    return e / e.sum(1, keepdims=True)


def setup_inputs():
    u = mx_kscale(C)
    return {"supports": bf(draw_supports()),
            "cand": bf(np.random.standard_normal((B, N, C)) * 0.7 * u),
            "c1": bf(np.random.standard_normal((B, N, C)) * 0.3 * u),
            "W_update": bf(np.random.standard_normal((KC, H)) * np.sqrt(2.0 / (KC + H)) / np.tile(u, CHEB)[:, None]),
            "b_update": bf(np.random.standard_normal(H) * 0.3),
            "r": bf(1.0 / (1.0 + np.exp(-np.random.standard_normal((B, N, H))))),
            "state": bf(np.random.standard_normal((B, N, H)))}


def reference(supports, cand, c1, W_update, b_update, r, state):
    c0, c1f = f64(cand), f64(c1)
    c2 = 2.0 * (mxq(f64(supports), 1, "e4m3") @ mxq(c1f, 1, "e4m3")) - c0
    xg = np.concatenate([c0, c1f, c2], -1)
    hc = np.tanh((mxq(xg, 2, "e4m3") @ mxq(f64(W_update), 0, "e4m3")) + f64(b_update))
    return f64(r) * f64(state) + (1.0 - f64(r)) * hc

@@ -1,0 +1,211 @@
+from contextlib import ExitStack
+
+import concourse.mybir as mybir
+from concourse.masks import make_identity
+
+F32 = mybir.dt.float32
+BF16 = mybir.dt.bfloat16
+U32 = mybir.dt.uint32
+U8 = mybir.dt.uint8
+FP8X4 = mybir.dt.float8_e4m3fn_x4
+ALU = mybir.AluOpType
+ACT = mybir.ActivationFunctionType
+
+P = 128
+PACK = 4
+B, N, C, H = 16, 512, 512, 128
+PARTS = 3
+NT = N // P
+GROUPED = N * PACK
+AHEAD = 3
+
+FLOPS = 2 * B * N * N * C + 2 * B * N * PARTS * C * H
+
+
+def tile_agcrncell_pc_t_kernel(tc, supports, cand, c1, W_update, b_update, r, state, out):
+    nc = tc.nc
+    with ExitStack() as stack:
+        const = stack.enter_context(tc.tile_pool(name="const", bufs=1))
+        big_in = stack.enter_context(tc.tile_pool(name="big_in", bufs=AHEAD + 1))
+        gate_in = stack.enter_context(tc.tile_pool(name="gate_in", bufs=AHEAD + 3))
+        work = stack.enter_context(tc.tile_pool(name="work", bufs=2))
+        tr_psum = stack.enter_context(tc.psum_pool(name="tr_psum", bufs=2))
+        hop_psum = stack.enter_context(tc.psum_pool(name="hop_psum", bufs=NT))
+        upd_psum = stack.enter_context(tc.psum_pool(name="upd_psum", bufs=1))
+        back_psum = stack.enter_context(tc.psum_pool(name="back_psum", bufs=1))
+        stack.enter_context(tc.manual_schedule())
+
+        c1_sb, cand_sb, r_sb, state_sb = {}, {}, {}, {}
+        c1_by_node, c1_codes, c1_scales = {}, {}, {}
+        cand_g, c1_g, c2_g, xg_codes, xg_scales = {}, {}, {}, {}, {}
+        hop_acc, hc_t, hc_bank, blend = {}, {}, {}, {}
+
+        def load(b):
+            c1_sb[b] = big_in.tile([P, NT, C], BF16, name="c1_sb")
+            nc.sync.dma_start(out=c1_sb[b][:], in_=c1[b].rearrange("(p i) c -> p i c", i=NT))
+            cand_sb[b] = big_in.tile([P, NT, C], BF16, name="cand_sb")
+            nc.sync.dma_start(out=cand_sb[b][:], in_=cand[b].rearrange("(p i) c -> p i c", i=NT))
+            r_sb[b] = gate_in.tile([P, NT, H], BF16, name="r_sb")
+            nc.sync.dma_start(out=r_sb[b][:], in_=r[b].rearrange("(p i) h -> p i h", i=NT))
+            state_sb[b] = gate_in.tile([P, NT, H], BF16, name="state_sb")
+            nc.sync.dma_start(out=state_sb[b][:], in_=state[b].rearrange("(p i) h -> p i h", i=NT))
+
+        def transpose_words(word_block, grouped):
+            grouped_words = grouped[:].bitcast(F32).rearrange("q (w u) -> q w u", u=2)
+            for half in range(2):
+                bank = tr_psum.tile([P, 2, 2 * P], F32, name="bank")
+                for il in range(2):
+                    for u in range(2):
+                        nc.tensor.transpose(bank[:, u, il * P : (il + 1) * P], word_block(2 * half + il, u), ident[:])
+                nc.scalar.copy(
+                    out=grouped_words[:, half * 2 * P : (half + 1) * 2 * P, :],
+                    in_=bank[:].rearrange("q u w -> q w u"),
+                )
+
+        def contiguous_words(x_sb):
+            words = x_sb[:].bitcast(F32)
+            return lambda i, u: words[:, i, u * P : (u + 1) * P]
+
+        def regroup_c1(b):
+            c1_by_node[b] = work.tile([P, GROUPED], BF16, name="c1_by_node", align_bytes=64)
+            dst = c1_by_node[b][:].rearrange("p (u e q j) -> p u e q j", u=2, e=2, j=PACK)
+            src = c1_sb[b][:].rearrange("p j (u q e) -> p u e q j", u=2, e=2)
+            for u in range(2):
+                nc.scalar.copy(out=dst[:, u], in_=src[:, u])
+
+        def transpose_inputs(b):
+            c1_g[b] = work.tile([P, GROUPED], BF16, name="c1_g", align_bytes=64)
+            transpose_words(contiguous_words(c1_sb[b]), c1_g[b])
+            cand_g[b] = work.tile([P, GROUPED], BF16, name="cand_g", align_bytes=64)
+            transpose_words(contiguous_words(cand_sb[b]), cand_g[b])
+
+        def quantise(codes, scales, grouped):
+            nc.vector.quantize_mx(out=codes.bitcast(FP8X4), scales=scales, in_=grouped)
+
+        def quantise_c1_by_node(b):
+            c1_codes[b] = work.tile([P, C], U32, name="c1_codes", align_bytes=64)
+            c1_scales[b] = work.tile([P, C], U8, name="c1_scales", align_bytes=64)
+            quantise(c1_codes[b][:], c1_scales[b][:], c1_by_node[b][:])
+
+        def quantise_cand_and_c1(b):
+            xg_codes[b] = work.tile([P, PARTS, N], U32, name="xg_codes", align_bytes=64)
+            xg_scales[b] = work.tile([P, PARTS, N], U8, name="xg_scales", align_bytes=64)
+            quantise(xg_codes[b][:, 0, :], xg_scales[b][:, 0, :], cand_g[b][:])
+            quantise(xg_codes[b][:, 1, :], xg_scales[b][:, 1, :], c1_g[b][:])
+
+        def hop_matmuls(b):
+            hop_acc[b] = []
+            for i in range(NT):
+                acc = hop_psum.tile([P, PACK, P], F32, name="acc")
+                for t in range(PACK):
+                    nc.tensor.matmul_mx(
+                        out=acc[:, t, :],
+                        lhsT=c1_codes[b][:, t * P : (t + 1) * P].bitcast(FP8X4),
+                        lhsT_scale=c1_scales[b][:, t * P : (t + 1) * P],
+                        rhs=sup_codes[:, i * P : (i + 1) * P].bitcast(FP8X4),
+                        rhs_scale=sup_scales[:, i * P : (i + 1) * P],
+                        start=True,
+                        stop=True,
+                    )
+                hop_acc[b].append(acc)
+            c2_g[b] = work.tile([P, GROUPED], BF16, name="c2_g", align_bytes=64)
+
+        def finish_c2(b, i):
+            cols = slice(i * P, (i + 1) * P)
+            nc.vector.scalar_tensor_tensor(
+                out=c2_g[b][:].rearrange("q (w t) -> q w t", t=PACK)[:, cols, :],
+                in0=hop_acc[b][i][:].rearrange("q t w -> q w t"),
+                scalar=2.0,
+                in1=cand_g[b][:].rearrange("q (w t) -> q w t", t=PACK)[:, cols, :],
+                op0=ALU.mult,
+                op1=ALU.subtract,
+            )
+
+        def update(b):
+            quantise(xg_codes[b][:, 2, :], xg_scales[b][:, 2, :], c2_g[b][:])
+            z = upd_psum.tile([P, N], F32, name="z")
+            for g in range(PARTS):
+                nc.tensor.matmul_mx(
+                    out=z[:],
+                    lhsT=w_codes[:, g, :].bitcast(FP8X4),
+                    lhsT_scale=w_scales[:, g, :],
+                    rhs=xg_codes[b][:, g, :].bitcast(FP8X4),
+                    rhs_scale=xg_scales[b][:, g, :],
+                    start=(g == 0),
+                    stop=(g == PARTS - 1),
+                )
+            hc_t[b] = work.tile([P, N], F32, name="hc_t")
+            nc.scalar.activation(out=hc_t[b][:], in_=z[:], func=ACT.Tanh, bias=bias_col[:, 0:1], scale=1.0)
+
+        def transpose_back(b):
+            hc_bank[b] = back_psum.tile([P, NT, H], F32, name="hc_bank")
+            for i in range(NT):
+                nc.tensor.transpose(hc_bank[b][:, i, :], hc_t[b][:, i * P : (i + 1) * P], ident[:])
+            blend[b] = work.tile([P, NT, H], F32, name="blend", bufs=3)
+
+        def blend_step(b, step):
+            if step == 0:
+                nc.vector.tensor_tensor(out=blend[b][:], in0=hc_bank[b][:], in1=state_sb[b][:], op=ALU.subtract)
+            elif step == 1:
+                nc.vector.scalar_tensor_tensor(
+                    out=blend[b][:], in0=r_sb[b][:], scalar=1.0, in1=blend[b][:], op0=ALU.subtract, op1=ALU.mult
+                )
+            else:
+                nc.vector.tensor_tensor(out=blend[b][:], in0=state_sb[b][:], in1=blend[b][:], op=ALU.subtract)
+                nc.sync.dma_start(out=out[b].rearrange("(p i) h -> p i h", i=NT), in_=blend[b][:])
+
+        sup_sb = const.tile([P, NT, N], BF16, name="sup_sb")
+        nc.sync.dma_start(out=sup_sb[:], in_=supports.rearrange("(p i) m -> p i m", i=NT))
+        load(0)
+        w_sb = const.tile([P, PARTS * PACK, H], BF16, name="w_sb")
+        nc.sync.dma_start(
+            out=w_sb[:].rearrange("q (a e) h -> q a e h", e=2),
+            in_=W_update.rearrange("(a q e) h -> q a e h", q=P, e=2),
+        )
+        bias_bf = const.tile([P, 1], BF16, name="bias_bf")
+        with nc.allow_non_contiguous_dma(reason="128 bias values, one to a partition"):
+            nc.sync.dma_start(out=bias_bf[:], in_=b_update.rearrange("(h o) -> h o", o=1))
+        for b in range(1, AHEAD):
+            load(b)
+
+        ident = const.tile([P, P], F32, name="ident")
+        make_identity(nc, ident[:])
+
+        sup_words = sup_sb[:].bitcast(F32).rearrange("p i (q s) -> p i q s", s=2)
+        sup_g = const.tile([P, GROUPED], BF16, name="sup_g", align_bytes=64)
+        transpose_words(lambda i, s: sup_words[:, i, :, s], sup_g)
+        regroup_c1(0)
+        transpose_inputs(0)
+        sup_codes = const.tile([P, N], U32, name="sup_codes", align_bytes=64)
+        sup_scales = const.tile([P, N], U8, name="sup_scales", align_bytes=64)
+        quantise(sup_codes[:], sup_scales[:], sup_g[:])
+
+        w_g = const.tile([P, PARTS, H, PACK], BF16, name="w_g", align_bytes=64)
+        nc.vector.tensor_copy(out=w_g[:], in_=w_sb[:].rearrange("q (g t) h -> q g h t", t=PACK))
+        bias_col = const.tile([P, 1], F32, name="bias_col")
+        nc.vector.tensor_copy(out=bias_col[:], in_=bias_bf[:])
+        w_codes = const.tile([P, PARTS, H], U32, name="w_codes", align_bytes=64)
+        w_scales = const.tile([P, PARTS, H], U8, name="w_scales", align_bytes=64)
+        for g in range(PARTS):
+            quantise(w_codes[:, g, :], w_scales[:, g, :], w_g[:, g].rearrange("q h t -> q (h t)"))
+
+        for k in range(B + 1):
+            if k + AHEAD < B:
+                load(k + AHEAD)
+            if k + 1 < B:
+                regroup_c1(k + 1)
+            if k >= 1:
+                update(k - 1)
+            if k < B:
+                quantise_c1_by_node(k)
+                hop_matmuls(k)
+                quantise_cand_and_c1(k)
+            if k >= 1:
+                transpose_back(k - 1)
+            if k + 1 < B:
+                transpose_inputs(k + 1)
+            for i in range(NT):
+                if k < B:
+                    finish_c2(k, i)
+                if k >= 1 and i >= 1:
+                    blend_step(k - 1, i - 1)

@@ -17,7 +17,7 @@ B, N, C, H = 16, 512, 512, 128
 PARTS = 3
 NT = N // P
 GROUPED = N * PACK
-AHEAD = 3
+AHEAD = 4
 
 FLOPS = 2 * B * N * N * C + 2 * B * N * PARTS * C * H
 
@@ -38,17 +38,17 @@ def tile_agcrncell_pc_t_kernel(tc, supports, cand, c1, W_update, b_update, r, st
         c1_sb, cand_sb, r_sb, state_sb = {}, {}, {}, {}
         c1_by_node, c1_codes, c1_scales = {}, {}, {}
         cand_g, c1_g, c2_g, xg_codes, xg_scales = {}, {}, {}, {}, {}
-        hop_acc, hc_t, hc_bank, blend = {}, {}, {}, {}
+        hop_acc, hc_t, hc_minus_state = {}, {}, {}
 
         def load(b):
             c1_sb[b] = big_in.tile([P, NT, C], BF16, name="c1_sb")
             nc.sync.dma_start(out=c1_sb[b][:], in_=c1[b].rearrange("(p i) c -> p i c", i=NT))
             cand_sb[b] = big_in.tile([P, NT, C], BF16, name="cand_sb")
             nc.sync.dma_start(out=cand_sb[b][:], in_=cand[b].rearrange("(p i) c -> p i c", i=NT))
-            r_sb[b] = gate_in.tile([P, NT, H], BF16, name="r_sb")
-            nc.sync.dma_start(out=r_sb[b][:], in_=r[b].rearrange("(p i) h -> p i h", i=NT))
-            state_sb[b] = gate_in.tile([P, NT, H], BF16, name="state_sb")
-            nc.sync.dma_start(out=state_sb[b][:], in_=state[b].rearrange("(p i) h -> p i h", i=NT))
+            r_sb[b] = gate_in.tile([P, NT * H], BF16, name="r_sb")
+            nc.sync.dma_start(out=r_sb[b][:], in_=r[b].rearrange("(p i) h -> p (i h)", i=NT))
+            state_sb[b] = gate_in.tile([P, NT * H], BF16, name="state_sb")
+            nc.sync.dma_start(out=state_sb[b][:], in_=state[b].rearrange("(p i) h -> p (i h)", i=NT))
 
         def transpose_words(word_block, grouped):
             grouped_words = grouped[:].bitcast(F32).rearrange("q (w u) -> q w u", u=2)
@@ -66,12 +66,12 @@ def tile_agcrncell_pc_t_kernel(tc, supports, cand, c1, W_update, b_update, r, st
             words = x_sb[:].bitcast(F32)
             return lambda i, u: words[:, i, u * P : (u + 1) * P]
 
-        def regroup_c1(b):
+        def regroup_c1(b, copy):
             c1_by_node[b] = work.tile([P, GROUPED], BF16, name="c1_by_node", align_bytes=64)
             dst = c1_by_node[b][:].rearrange("p (u e q j) -> p u e q j", u=2, e=2, j=PACK)
             src = c1_sb[b][:].rearrange("p j (u q e) -> p u e q j", u=2, e=2)
             for u in range(2):
-                nc.scalar.copy(out=dst[:, u], in_=src[:, u])
+                copy(out=dst[:, u], in_=src[:, u])
 
         def transpose_inputs(b):
             c1_g[b] = work.tile([P, GROUPED], BF16, name="c1_g", align_bytes=64)
@@ -86,12 +86,6 @@ def tile_agcrncell_pc_t_kernel(tc, supports, cand, c1, W_update, b_update, r, st
             c1_codes[b] = work.tile([P, C], U32, name="c1_codes", align_bytes=64)
             c1_scales[b] = work.tile([P, C], U8, name="c1_scales", align_bytes=64)
             quantise(c1_codes[b][:], c1_scales[b][:], c1_by_node[b][:])
-
-        def quantise_cand_and_c1(b):
-            xg_codes[b] = work.tile([P, PARTS, N], U32, name="xg_codes", align_bytes=64)
-            xg_scales[b] = work.tile([P, PARTS, N], U8, name="xg_scales", align_bytes=64)
-            quantise(xg_codes[b][:, 0, :], xg_scales[b][:, 0, :], cand_g[b][:])
-            quantise(xg_codes[b][:, 1, :], xg_scales[b][:, 1, :], c1_g[b][:])
 
         def hop_matmuls(b):
             hop_acc[b] = []
@@ -108,21 +102,24 @@ def tile_agcrncell_pc_t_kernel(tc, supports, cand, c1, W_update, b_update, r, st
                         stop=True,
                     )
                 hop_acc[b].append(acc)
+
+        def finish_c2(b):
             c2_g[b] = work.tile([P, GROUPED], BF16, name="c2_g", align_bytes=64)
+            for i in range(NT):
+                cols = slice(i * P, (i + 1) * P)
+                nc.vector.scalar_tensor_tensor(
+                    out=c2_g[b][:].rearrange("q (w t) -> q w t", t=PACK)[:, cols, :],
+                    in0=hop_acc[b][i][:].rearrange("q t w -> q w t"),
+                    scalar=2.0,
+                    in1=cand_g[b][:].rearrange("q (w t) -> q w t", t=PACK)[:, cols, :],
+                    op0=ALU.mult,
+                    op1=ALU.subtract,
+                )
 
-        def finish_c2(b, i):
-            cols = slice(i * P, (i + 1) * P)
-            nc.vector.scalar_tensor_tensor(
-                out=c2_g[b][:].rearrange("q (w t) -> q w t", t=PACK)[:, cols, :],
-                in0=hop_acc[b][i][:].rearrange("q t w -> q w t"),
-                scalar=2.0,
-                in1=cand_g[b][:].rearrange("q (w t) -> q w t", t=PACK)[:, cols, :],
-                op0=ALU.mult,
-                op1=ALU.subtract,
-            )
+        def quantise_xg(b, g, grouped):
+            quantise(xg_codes[b][:, g, :], xg_scales[b][:, g, :], grouped[b][:])
 
-        def update(b):
-            quantise(xg_codes[b][:, 2, :], xg_scales[b][:, 2, :], c2_g[b][:])
+        def update_matmuls(b):
             z = upd_psum.tile([P, N], F32, name="z")
             for g in range(PARTS):
                 nc.tensor.matmul_mx(
@@ -138,21 +135,26 @@ def tile_agcrncell_pc_t_kernel(tc, supports, cand, c1, W_update, b_update, r, st
             nc.scalar.activation(out=hc_t[b][:], in_=z[:], func=ACT.Tanh, bias=bias_col[:, 0:1], scale=1.0)
 
         def transpose_back(b):
-            hc_bank[b] = back_psum.tile([P, NT, H], F32, name="hc_bank")
+            hc_minus_state[b] = back_psum.tile([P, NT * H], F32, name="hc_minus_state")
             for i in range(NT):
-                nc.tensor.transpose(hc_bank[b][:, i, :], hc_t[b][:, i * P : (i + 1) * P], ident[:])
-            blend[b] = work.tile([P, NT, H], F32, name="blend", bufs=3)
-
-        def blend_step(b, step):
-            if step == 0:
-                nc.vector.tensor_tensor(out=blend[b][:], in0=hc_bank[b][:], in1=state_sb[b][:], op=ALU.subtract)
-            elif step == 1:
-                nc.vector.scalar_tensor_tensor(
-                    out=blend[b][:], in0=r_sb[b][:], scalar=1.0, in1=blend[b][:], op0=ALU.subtract, op1=ALU.mult
+                nc.tensor.matmul(
+                    out=hc_minus_state[b][:, i * H : (i + 1) * H],
+                    lhsT=hc_t[b][:, i * P : (i + 1) * P],
+                    rhs=ident[:],
+                    is_transpose=True,
+                    start=(i == 0),
+                    stop=False,
                 )
-            else:
-                nc.vector.tensor_tensor(out=blend[b][:], in0=state_sb[b][:], in1=blend[b][:], op=ALU.subtract)
-                nc.sync.dma_start(out=out[b].rearrange("(p i) h -> p i h", i=NT), in_=blend[b][:])
+            nc.tensor.matmul(out=hc_minus_state[b][:], lhsT=minus_ident[:], rhs=state_sb[b][:], start=False, stop=True)
+
+        def blend(b):
+            step = work.tile([P, NT * H], F32, name="step")
+            nc.vector.scalar_tensor_tensor(
+                out=step[:], in0=r_sb[b][:], scalar=1.0, in1=hc_minus_state[b][:], op0=ALU.subtract, op1=ALU.mult
+            )
+            result = work.tile([P, NT * H], F32, name="result", bufs=3)
+            nc.gpsimd.tensor_tensor(out=result[:], in0=state_sb[b][:], in1=step[:], op=ALU.subtract)
+            nc.sync.dma_start(out=out[b].rearrange("(p i) h -> p (i h)", i=NT), in_=result[:])
 
         sup_sb = const.tile([P, NT, N], BF16, name="sup_sb")
         nc.sync.dma_start(out=sup_sb[:], in_=supports.rearrange("(p i) m -> p i m", i=NT))
@@ -170,15 +172,19 @@ def tile_agcrncell_pc_t_kernel(tc, supports, cand, c1, W_update, b_update, r, st
 
         ident = const.tile([P, P], F32, name="ident")
         make_identity(nc, ident[:])
+        minus_ident = const.tile([P, P], BF16, name="minus_ident")
+        nc.vector.tensor_scalar_mul(out=minus_ident[:], in0=ident[:], scalar1=-1.0)
 
         sup_words = sup_sb[:].bitcast(F32).rearrange("p i (q s) -> p i q s", s=2)
         sup_g = const.tile([P, GROUPED], BF16, name="sup_g", align_bytes=64)
         transpose_words(lambda i, s: sup_words[:, i, :, s], sup_g)
-        regroup_c1(0)
+        regroup_c1(0, nc.vector.tensor_copy)
         transpose_inputs(0)
         sup_codes = const.tile([P, N], U32, name="sup_codes", align_bytes=64)
         sup_scales = const.tile([P, N], U8, name="sup_scales", align_bytes=64)
         quantise(sup_codes[:], sup_scales[:], sup_g[:])
+        quantise_c1_by_node(0)
+        regroup_c1(1, nc.vector.tensor_copy)
 
         w_g = const.tile([P, PARTS, H, PACK], BF16, name="w_g", align_bytes=64)
         nc.vector.tensor_copy(out=w_g[:], in_=w_sb[:].rearrange("q (g t) h -> q g h t", t=PACK))
@@ -192,20 +198,26 @@ def tile_agcrncell_pc_t_kernel(tc, supports, cand, c1, W_update, b_update, r, st
         for k in range(B + 1):
             if k + AHEAD < B:
                 load(k + AHEAD)
-            if k + 1 < B:
-                regroup_c1(k + 1)
-            if k >= 1:
-                update(k - 1)
             if k < B:
-                quantise_c1_by_node(k)
                 hop_matmuls(k)
-                quantise_cand_and_c1(k)
             if k >= 1:
-                transpose_back(k - 1)
+                update_matmuls(k - 1)
+            if k < B:
+                finish_c2(k)
             if k + 1 < B:
                 transpose_inputs(k + 1)
-            for i in range(NT):
-                if k < B:
-                    finish_c2(k, i)
-                if k >= 1 and i >= 1:
-                    blend_step(k - 1, i - 1)
+            if k >= 1:
+                transpose_back(k - 1)
+            if k + 2 < B:
+                regroup_c1(k + 2, nc.scalar.copy)
+            if k < B:
+                xg_codes[k] = work.tile([P, PARTS, N], U32, name="xg_codes", align_bytes=64)
+                xg_scales[k] = work.tile([P, PARTS, N], U8, name="xg_scales", align_bytes=64)
+                quantise_xg(k, 0, cand_g)
+                quantise_xg(k, 1, c1_g)
+            if k + 1 < B:
+                quantise_c1_by_node(k + 1)
+            if k < B:
+                quantise_xg(k, 2, c2_g)
+            if k >= 1:
+                blend(k - 1)

@@ -29,15 +29,14 @@ def tile_agcrncell_pc_t_kernel(tc, supports, cand, c1, W_update, b_update, r, st
         big_in = stack.enter_context(tc.tile_pool(name="big_in", bufs=AHEAD + 1))
         gate_in = stack.enter_context(tc.tile_pool(name="gate_in", bufs=AHEAD + 3))
         work = stack.enter_context(tc.tile_pool(name="work", bufs=2))
-        tr_psum = stack.enter_context(tc.psum_pool(name="tr_psum", bufs=2))
+        tr_psum = stack.enter_context(tc.psum_pool(name="tr_psum", bufs=3))
         hop_psum = stack.enter_context(tc.psum_pool(name="hop_psum", bufs=NT))
-        upd_psum = stack.enter_context(tc.psum_pool(name="upd_psum", bufs=1))
-        back_psum = stack.enter_context(tc.psum_pool(name="back_psum", bufs=1))
+        end_psum = stack.enter_context(tc.psum_pool(name="end_psum", bufs=1))
         stack.enter_context(tc.manual_schedule())
 
         c1_sb, cand_sb, r_sb, state_sb = {}, {}, {}, {}
         c1_by_node, c1_codes, c1_scales = {}, {}, {}
-        cand_g, c1_g, c2_g, xg_codes, xg_scales = {}, {}, {}, {}, {}
+        given_g, c2_g, xg_codes, xg_scales = {}, {}, {}, {}
         hop_acc, hc_t, hc_minus_state = {}, {}, {}
 
         def load(b):
@@ -51,7 +50,7 @@ def tile_agcrncell_pc_t_kernel(tc, supports, cand, c1, W_update, b_update, r, st
             nc.sync.dma_start(out=state_sb[b][:], in_=state[b].rearrange("(p i) h -> p (i h)", i=NT))
 
         def transpose_words(word_block, grouped):
-            grouped_words = grouped[:].bitcast(F32).rearrange("q (w u) -> q w u", u=2)
+            grouped_words = grouped.bitcast(F32).rearrange("q (w u) -> q w u", u=2)
             for half in range(2):
                 bank = tr_psum.tile([P, 2, 2 * P], F32, name="bank")
                 for il in range(2):
@@ -66,18 +65,21 @@ def tile_agcrncell_pc_t_kernel(tc, supports, cand, c1, W_update, b_update, r, st
             words = x_sb[:].bitcast(F32)
             return lambda i, u: words[:, i, u * P : (u + 1) * P]
 
-        def regroup_c1(b, copy):
+        def gpsimd_copy(out, in_):
+            nc.gpsimd.tensor_scalar(out=out, in0=in_, scalar1=1.0, scalar2=0.0, op0=ALU.mult, op1=ALU.add)
+
+        def regroup_c1(b, copy, last_copy):
             c1_by_node[b] = work.tile([P, GROUPED], BF16, name="c1_by_node", align_bytes=64)
-            dst = c1_by_node[b][:].rearrange("p (u e q j) -> p u e q j", u=2, e=2, j=PACK)
+            dst = c1_by_node[b][:].rearrange("p (t q j) -> p t q j", t=PACK, j=PACK)
             src = c1_sb[b][:].rearrange("p j (u q e) -> p u e q j", u=2, e=2)
-            for u in range(2):
-                copy(out=dst[:, u], in_=src[:, u])
+            for t in range(PACK - 1):
+                copy(out=dst[:, t], in_=src[:, t // 2, t % 2])
+            last_copy(out=dst[:, PACK - 1], in_=src[:, 1, 1])
 
         def transpose_inputs(b):
-            c1_g[b] = work.tile([P, GROUPED], BF16, name="c1_g", align_bytes=64)
-            transpose_words(contiguous_words(c1_sb[b]), c1_g[b])
-            cand_g[b] = work.tile([P, GROUPED], BF16, name="cand_g", align_bytes=64)
-            transpose_words(contiguous_words(cand_sb[b]), cand_g[b])
+            given_g[b] = work.tile([P, 2, GROUPED], BF16, name="given_g", align_bytes=64)
+            transpose_words(contiguous_words(cand_sb[b]), given_g[b][:, 0, :])
+            transpose_words(contiguous_words(c1_sb[b]), given_g[b][:, 1, :])
 
         def quantise(codes, scales, grouped):
             nc.vector.quantize_mx(out=codes.bitcast(FP8X4), scales=scales, in_=grouped)
@@ -111,23 +113,28 @@ def tile_agcrncell_pc_t_kernel(tc, supports, cand, c1, W_update, b_update, r, st
                     out=c2_g[b][:].rearrange("q (w t) -> q w t", t=PACK)[:, cols, :],
                     in0=hop_acc[b][i][:].rearrange("q t w -> q w t"),
                     scalar=2.0,
-                    in1=cand_g[b][:].rearrange("q (w t) -> q w t", t=PACK)[:, cols, :],
+                    in1=given_g[b][:, 0, :].rearrange("q (w t) -> q w t", t=PACK)[:, cols, :],
                     op0=ALU.mult,
                     op1=ALU.subtract,
                 )
 
-        def quantise_xg(b, g, grouped):
-            quantise(xg_codes[b][:, g, :], xg_scales[b][:, g, :], grouped[b][:])
+        def quantise_cand_and_c1(b):
+            xg_codes[b] = work.tile([P, PARTS * N], U32, name="xg_codes", align_bytes=64)
+            xg_scales[b] = work.tile([P, PARTS * N], U8, name="xg_scales", align_bytes=64)
+            quantise(xg_codes[b][:, : 2 * N], xg_scales[b][:, : 2 * N], given_g[b][:].rearrange("q g x -> q (g x)"))
+
+        def quantise_c2(b):
+            quantise(xg_codes[b][:, 2 * N :], xg_scales[b][:, 2 * N :], c2_g[b][:])
 
         def update_matmuls(b):
-            z = upd_psum.tile([P, N], F32, name="z")
+            z = end_psum.tile([P, N], F32, name="z", tag="end")
             for g in range(PARTS):
                 nc.tensor.matmul_mx(
                     out=z[:],
                     lhsT=w_codes[:, g, :].bitcast(FP8X4),
                     lhsT_scale=w_scales[:, g, :],
-                    rhs=xg_codes[b][:, g, :].bitcast(FP8X4),
-                    rhs_scale=xg_scales[b][:, g, :],
+                    rhs=xg_codes[b][:, g * N : (g + 1) * N].bitcast(FP8X4),
+                    rhs_scale=xg_scales[b][:, g * N : (g + 1) * N],
                     start=(g == 0),
                     stop=(g == PARTS - 1),
                 )
@@ -135,7 +142,7 @@ def tile_agcrncell_pc_t_kernel(tc, supports, cand, c1, W_update, b_update, r, st
             nc.scalar.activation(out=hc_t[b][:], in_=z[:], func=ACT.Tanh, bias=bias_col[:, 0:1], scale=1.0)
 
         def transpose_back(b):
-            hc_minus_state[b] = back_psum.tile([P, NT * H], F32, name="hc_minus_state")
+            hc_minus_state[b] = end_psum.tile([P, NT * H], F32, name="hc_minus_state", tag="end")
             for i in range(NT):
                 nc.tensor.matmul(
                     out=hc_minus_state[b][:, i * H : (i + 1) * H],
@@ -177,17 +184,17 @@ def tile_agcrncell_pc_t_kernel(tc, supports, cand, c1, W_update, b_update, r, st
 
         sup_words = sup_sb[:].bitcast(F32).rearrange("p i (q s) -> p i q s", s=2)
         sup_g = const.tile([P, GROUPED], BF16, name="sup_g", align_bytes=64)
-        transpose_words(lambda i, s: sup_words[:, i, :, s], sup_g)
-        regroup_c1(0, nc.vector.tensor_copy)
+        transpose_words(lambda i, s: sup_words[:, i, :, s], sup_g[:])
+        regroup_c1(0, nc.vector.tensor_copy, nc.vector.tensor_copy)
         transpose_inputs(0)
         sup_codes = const.tile([P, N], U32, name="sup_codes", align_bytes=64)
         sup_scales = const.tile([P, N], U8, name="sup_scales", align_bytes=64)
         quantise(sup_codes[:], sup_scales[:], sup_g[:])
         quantise_c1_by_node(0)
-        regroup_c1(1, nc.vector.tensor_copy)
+        regroup_c1(1, nc.scalar.copy, gpsimd_copy)
 
         w_g = const.tile([P, PARTS, H, PACK], BF16, name="w_g", align_bytes=64)
-        nc.vector.tensor_copy(out=w_g[:], in_=w_sb[:].rearrange("q (g t) h -> q g h t", t=PACK))
+        gpsimd_copy(out=w_g[:], in_=w_sb[:].rearrange("q (g t) h -> q g h t", t=PACK))
         bias_col = const.tile([P, 1], F32, name="bias_col")
         nc.vector.tensor_copy(out=bias_col[:], in_=bias_bf[:])
         w_codes = const.tile([P, PARTS, H], U32, name="w_codes", align_bytes=64)
@@ -209,15 +216,12 @@ def tile_agcrncell_pc_t_kernel(tc, supports, cand, c1, W_update, b_update, r, st
             if k >= 1:
                 transpose_back(k - 1)
             if k + 2 < B:
-                regroup_c1(k + 2, nc.scalar.copy)
+                regroup_c1(k + 2, nc.scalar.copy, gpsimd_copy)
             if k < B:
-                xg_codes[k] = work.tile([P, PARTS, N], U32, name="xg_codes", align_bytes=64)
-                xg_scales[k] = work.tile([P, PARTS, N], U8, name="xg_scales", align_bytes=64)
-                quantise_xg(k, 0, cand_g)
-                quantise_xg(k, 1, c1_g)
+                quantise_cand_and_c1(k)
             if k + 1 < B:
                 quantise_c1_by_node(k + 1)
             if k < B:
-                quantise_xg(k, 2, c2_g)
+                quantise_c2(k)
             if k >= 1:
                 blend(k - 1)

@@ -76,9 +76,11 @@ def tile_agcrncell_pc_t_kernel(tc, supports, cand, c1, W_update, b_update, r, st
                 copy(out=dst[:, t], in_=src[:, t // 2, t % 2])
             last_copy(out=dst[:, PACK - 1], in_=src[:, 1, 1])
 
-        def transpose_inputs(b):
+        def transpose_cand(b):
             given_g[b] = work.tile([P, 2, GROUPED], BF16, name="given_g", align_bytes=64)
             transpose_words(contiguous_words(cand_sb[b]), given_g[b][:, 0, :])
+
+        def transpose_c1(b):
             transpose_words(contiguous_words(c1_sb[b]), given_g[b][:, 1, :])
 
         def quantise(codes, scales, grouped):
@@ -186,7 +188,8 @@ def tile_agcrncell_pc_t_kernel(tc, supports, cand, c1, W_update, b_update, r, st
         sup_g = const.tile([P, GROUPED], BF16, name="sup_g", align_bytes=64)
         transpose_words(lambda i, s: sup_words[:, i, :, s], sup_g[:])
         regroup_c1(0, nc.vector.tensor_copy, nc.vector.tensor_copy)
-        transpose_inputs(0)
+        transpose_cand(0)
+        transpose_c1(0)
         sup_codes = const.tile([P, N], U32, name="sup_codes", align_bytes=64)
         sup_scales = const.tile([P, N], U8, name="sup_scales", align_bytes=64)
         quantise(sup_codes[:], sup_scales[:], sup_g[:])
@@ -194,7 +197,7 @@ def tile_agcrncell_pc_t_kernel(tc, supports, cand, c1, W_update, b_update, r, st
         regroup_c1(1, nc.scalar.copy, gpsimd_copy)
 
         w_g = const.tile([P, PARTS, H, PACK], BF16, name="w_g", align_bytes=64)
-        gpsimd_copy(out=w_g[:], in_=w_sb[:].rearrange("q (g t) h -> q g h t", t=PACK))
+        nc.vector.tensor_copy(out=w_g[:], in_=w_sb[:].rearrange("q (g t) h -> q g h t", t=PACK))
         bias_col = const.tile([P, 1], F32, name="bias_col")
         nc.vector.tensor_copy(out=bias_col[:], in_=bias_bf[:])
         w_codes = const.tile([P, PARTS, H], U32, name="w_codes", align_bytes=64)
@@ -207,12 +210,13 @@ def tile_agcrncell_pc_t_kernel(tc, supports, cand, c1, W_update, b_update, r, st
                 load(k + AHEAD)
             if k < B:
                 hop_matmuls(k)
-            if k >= 1:
-                update_matmuls(k - 1)
-            if k < B:
                 finish_c2(k)
             if k + 1 < B:
-                transpose_inputs(k + 1)
+                transpose_cand(k + 1)
+            if k >= 1:
+                update_matmuls(k - 1)
+            if k + 1 < B:
+                transpose_c1(k + 1)
             if k >= 1:
                 transpose_back(k - 1)
             if k + 2 < B:

@@ -162,7 +162,8 @@ def tile_agcrncell_pc_t_kernel(tc, supports, cand, c1, W_update, b_update, r, st
                 out=step[:], in0=r_sb[b][:], scalar=1.0, in1=hc_minus_state[b][:], op0=ALU.subtract, op1=ALU.mult
             )
             result = work.tile([P, NT * H], F32, name="result", bufs=3)
-            nc.gpsimd.tensor_tensor(out=result[:], in0=state_sb[b][:], in1=step[:], op=ALU.subtract)
+            subtract = nc.vector.tensor_tensor if b == B - 1 else nc.gpsimd.tensor_tensor
+            subtract(out=result[:], in0=state_sb[b][:], in1=step[:], op=ALU.subtract)
             nc.sync.dma_start(out=out[b].rearrange("(p i) h -> p (i h)", i=NT), in_=result[:])
 
         sup_sb = const.tile([P, NT, N], BF16, name="sup_sb")
@@ -175,7 +176,7 @@ def tile_agcrncell_pc_t_kernel(tc, supports, cand, c1, W_update, b_update, r, st
         )
         bias_bf = const.tile([P, 1], BF16, name="bias_bf")
         with nc.allow_non_contiguous_dma(reason="128 bias values, one to a partition"):
-            nc.sync.dma_start(out=bias_bf[:], in_=b_update.rearrange("(h o) -> h o", o=1))
+            nc.scalar.dma_start(out=bias_bf[:], in_=b_update.rearrange("(h o) -> h o", o=1))
         for b in range(1, AHEAD):
             load(b)
 
@@ -192,8 +193,8 @@ def tile_agcrncell_pc_t_kernel(tc, supports, cand, c1, W_update, b_update, r, st
         transpose_c1(0)
         sup_codes = const.tile([P, N], U32, name="sup_codes", align_bytes=64)
         sup_scales = const.tile([P, N], U8, name="sup_scales", align_bytes=64)
-        quantise(sup_codes[:], sup_scales[:], sup_g[:])
         quantise_c1_by_node(0)
+        quantise(sup_codes[:], sup_scales[:], sup_g[:])
         regroup_c1(1, nc.scalar.copy, gpsimd_copy)
 
         w_g = const.tile([P, PARTS, H, PACK], BF16, name="w_g", align_bytes=64)
@@ -221,11 +222,10 @@ def tile_agcrncell_pc_t_kernel(tc, supports, cand, c1, W_update, b_update, r, st
                 transpose_back(k - 1)
             if k + 2 < B:
                 regroup_c1(k + 2, nc.scalar.copy, gpsimd_copy)
-            if k < B:
-                quantise_cand_and_c1(k)
             if k + 1 < B:
                 quantise_c1_by_node(k + 1)
             if k < B:
+                quantise_cand_and_c1(k)
                 quantise_c2(k)
             if k >= 1:
                 blend(k - 1)

@@ -70,8 +70,8 @@ def tile_agcrncell_pc_t_kernel(tc, supports, cand, c1, W_update, b_update, r, st
 
         def regroup_c1(b, copy, last_copy):
             c1_by_node[b] = work.tile([P, GROUPED], BF16, name="c1_by_node", align_bytes=64)
-            dst = c1_by_node[b][:].rearrange("p (t q j) -> p t q j", t=PACK, j=PACK)
-            src = c1_sb[b][:].rearrange("p j (u q e) -> p u e q j", u=2, e=2)
+            dst = c1_by_node[b][:].rearrange("p (t q f j) -> p t q j f", t=PACK, f=4, j=PACK)
+            src = c1_sb[b][:].rearrange("p j (u q f e) -> p u e q j f", u=2, f=4, e=2)
             for t in range(PACK - 1):
                 copy(out=dst[:, t], in_=src[:, t // 2, t % 2])
             last_copy(out=dst[:, PACK - 1], in_=src[:, 1, 1])

@@ -37,17 +37,26 @@ def tile_agcrncell_pc_t_kernel(tc, supports, cand, c1, W_update, b_update, r, st
         c1_sb, cand_sb, r_sb, state_sb = {}, {}, {}, {}
         c1_by_node, c1_codes, c1_scales = {}, {}, {}
         given_g, c2_g, xg_codes, xg_scales = {}, {}, {}, {}
-        hop_acc, hc_t, hc_minus_state = {}, {}, {}
+        hop_acc = {}
 
-        def load(b):
+        def load_c1(b):
             c1_sb[b] = big_in.tile([P, NT, C], BF16, name="c1_sb")
             nc.sync.dma_start(out=c1_sb[b][:], in_=c1[b].rearrange("(p i) c -> p i c", i=NT))
+
+        def load_cand(b):
             cand_sb[b] = big_in.tile([P, NT, C], BF16, name="cand_sb")
             nc.sync.dma_start(out=cand_sb[b][:], in_=cand[b].rearrange("(p i) c -> p i c", i=NT))
+
+        def load_gates(b):
             r_sb[b] = gate_in.tile([P, NT * H], BF16, name="r_sb")
             nc.sync.dma_start(out=r_sb[b][:], in_=r[b].rearrange("(p i) h -> p (i h)", i=NT))
             state_sb[b] = gate_in.tile([P, NT * H], BF16, name="state_sb")
             nc.sync.dma_start(out=state_sb[b][:], in_=state[b].rearrange("(p i) h -> p (i h)", i=NT))
+
+        def load(b):
+            load_c1(b)
+            load_cand(b)
+            load_gates(b)
 
         def transpose_words(word_block, grouped):
             grouped_words = grouped.bitcast(F32).rearrange("q (w u) -> q w u", u=2)
@@ -68,13 +77,12 @@ def tile_agcrncell_pc_t_kernel(tc, supports, cand, c1, W_update, b_update, r, st
         def gpsimd_copy(out, in_):
             nc.gpsimd.tensor_scalar(out=out, in0=in_, scalar1=1.0, scalar2=0.0, op0=ALU.mult, op1=ALU.add)
 
-        def regroup_c1(b, copy, last_copy):
+        def regroup_c1(b, copies):
             c1_by_node[b] = work.tile([P, GROUPED], BF16, name="c1_by_node", align_bytes=64)
             dst = c1_by_node[b][:].rearrange("p (t q f j) -> p t q j f", t=PACK, f=4, j=PACK)
             src = c1_sb[b][:].rearrange("p j (u q f e) -> p u e q j f", u=2, f=4, e=2)
-            for t in range(PACK - 1):
+            for t, copy in enumerate(copies):
                 copy(out=dst[:, t], in_=src[:, t // 2, t % 2])
-            last_copy(out=dst[:, PACK - 1], in_=src[:, 1, 1])
 
         def transpose_cand(b):
             given_g[b] = work.tile([P, 2, GROUPED], BF16, name="given_g", align_bytes=64)
@@ -107,9 +115,10 @@ def tile_agcrncell_pc_t_kernel(tc, supports, cand, c1, W_update, b_update, r, st
                     )
                 hop_acc[b].append(acc)
 
-        def finish_c2(b):
-            c2_g[b] = work.tile([P, GROUPED], BF16, name="c2_g", align_bytes=64)
-            for i in range(NT):
+        def finish_c2(b, tiles):
+            if b not in c2_g:
+                c2_g[b] = work.tile([P, GROUPED], BF16, name="c2_g", align_bytes=64)
+            for i in tiles:
                 cols = slice(i * P, (i + 1) * P)
                 nc.vector.scalar_tensor_tensor(
                     out=c2_g[b][:].rearrange("q (w t) -> q w t", t=PACK)[:, cols, :],
@@ -125,50 +134,57 @@ def tile_agcrncell_pc_t_kernel(tc, supports, cand, c1, W_update, b_update, r, st
             xg_scales[b] = work.tile([P, PARTS * N], U8, name="xg_scales", align_bytes=64)
             quantise(xg_codes[b][:, : 2 * N], xg_scales[b][:, : 2 * N], given_g[b][:].rearrange("q g x -> q (g x)"))
 
-        def quantise_c2(b):
-            quantise(xg_codes[b][:, 2 * N :], xg_scales[b][:, 2 * N :], c2_g[b][:])
+        def quantise_c2(b, tiles):
+            words = slice(2 * N + tiles[0] * P, 2 * N + (tiles[-1] + 1) * P)
+            grouped = c2_g[b][:, tiles[0] * P * PACK : (tiles[-1] + 1) * P * PACK]
+            quantise(xg_codes[b][:, words], xg_scales[b][:, words], grouped)
 
-        def update_matmuls(b):
-            z = end_psum.tile([P, N], F32, name="z", tag="end")
-            for g in range(PARTS):
+        def update_matmuls(b, z, parts, tiles):
+            for g in parts:
+                words = slice(g * N + tiles[0] * P, g * N + (tiles[-1] + 1) * P)
                 nc.tensor.matmul_mx(
-                    out=z[:],
+                    out=z,
                     lhsT=w_codes[:, g, :].bitcast(FP8X4),
                     lhsT_scale=w_scales[:, g, :],
-                    rhs=xg_codes[b][:, g * N : (g + 1) * N].bitcast(FP8X4),
-                    rhs_scale=xg_scales[b][:, g * N : (g + 1) * N],
+                    rhs=xg_codes[b][:, words].bitcast(FP8X4),
+                    rhs_scale=xg_scales[b][:, words],
                     start=(g == 0),
                     stop=(g == PARTS - 1),
                 )
-            hc_t[b] = work.tile([P, N], F32, name="hc_t")
-            nc.scalar.activation(out=hc_t[b][:], in_=z[:], func=ACT.Tanh, bias=bias_col[:, 0:1], scale=1.0)
 
-        def transpose_back(b):
-            hc_minus_state[b] = end_psum.tile([P, NT * H], F32, name="hc_minus_state", tag="end")
-            for i in range(NT):
+        def squash(z, width):
+            hc_t = work.tile([P, width], F32, name="hc_t")
+            nc.scalar.activation(out=hc_t[:], in_=z, func=ACT.Tanh, bias=bias_col[:, 0:1], scale=1.0)
+            return hc_t
+
+        def transpose_back(b, hc_t, bank, tiles):
+            for n, i in enumerate(tiles):
                 nc.tensor.matmul(
-                    out=hc_minus_state[b][:, i * H : (i + 1) * H],
-                    lhsT=hc_t[b][:, i * P : (i + 1) * P],
+                    out=bank[:, n * H : (n + 1) * H],
+                    lhsT=hc_t[:, n * P : (n + 1) * P],
                     rhs=ident[:],
                     is_transpose=True,
-                    start=(i == 0),
+                    start=(n == 0),
                     stop=False,
                 )
-            nc.tensor.matmul(out=hc_minus_state[b][:], lhsT=minus_ident[:], rhs=state_sb[b][:], start=False, stop=True)
+            cols = slice(tiles[0] * H, (tiles[-1] + 1) * H)
+            nc.tensor.matmul(out=bank, lhsT=minus_ident[:], rhs=state_sb[b][:, cols], start=False, stop=True)
 
-        def blend(b):
-            step = work.tile([P, NT * H], F32, name="step")
+        def blend(b, bank, tiles, subtract):
+            cols = slice(tiles[0] * H, (tiles[-1] + 1) * H)
+            width = len(tiles) * H
+            step = work.tile([P, width], F32, name="step")
             nc.vector.scalar_tensor_tensor(
-                out=step[:], in0=r_sb[b][:], scalar=1.0, in1=hc_minus_state[b][:], op0=ALU.subtract, op1=ALU.mult
+                out=step[:], in0=r_sb[b][:, cols], scalar=1.0, in1=bank, op0=ALU.subtract, op1=ALU.mult
             )
-            result = work.tile([P, NT * H], F32, name="result", bufs=3)
-            subtract = nc.vector.tensor_tensor if b == B - 1 else nc.gpsimd.tensor_tensor
-            subtract(out=result[:], in0=state_sb[b][:], in1=step[:], op=ALU.subtract)
-            nc.sync.dma_start(out=out[b].rearrange("(p i) h -> p (i h)", i=NT), in_=result[:])
+            result = work.tile([P, width], F32, name="result", bufs=6)
+            subtract(out=result[:], in0=state_sb[b][:, cols], in1=step[:], op=ALU.subtract)
+            rows = out[b].rearrange("(p i) h -> p (i h)", i=NT)
+            nc.sync.dma_start(out=rows[:, cols], in_=result[:])
 
+        load_c1(0)
         sup_sb = const.tile([P, NT, N], BF16, name="sup_sb")
         nc.sync.dma_start(out=sup_sb[:], in_=supports.rearrange("(p i) m -> p i m", i=NT))
-        load(0)
         w_sb = const.tile([P, PARTS * PACK, H], BF16, name="w_sb")
         nc.sync.dma_start(
             out=w_sb[:].rearrange("q (a e) h -> q a e h", e=2),
@@ -177,7 +193,12 @@ def tile_agcrncell_pc_t_kernel(tc, supports, cand, c1, W_update, b_update, r, st
         bias_bf = const.tile([P, 1], BF16, name="bias_bf")
         with nc.allow_non_contiguous_dma(reason="128 bias values, one to a partition"):
             nc.scalar.dma_start(out=bias_bf[:], in_=b_update.rearrange("(h o) -> h o", o=1))
-        for b in range(1, AHEAD):
+        load_cand(0)
+        load_c1(1)
+        load_cand(1)
+        load_gates(0)
+        load_gates(1)
+        for b in range(2, AHEAD):
             load(b)
 
         ident = const.tile([P, P], F32, name="ident")
@@ -188,44 +209,83 @@ def tile_agcrncell_pc_t_kernel(tc, supports, cand, c1, W_update, b_update, r, st
         sup_words = sup_sb[:].bitcast(F32).rearrange("p i (q s) -> p i q s", s=2)
         sup_g = const.tile([P, GROUPED], BF16, name="sup_g", align_bytes=64)
         transpose_words(lambda i, s: sup_words[:, i, :, s], sup_g[:])
-        regroup_c1(0, nc.vector.tensor_copy, nc.vector.tensor_copy)
+        regroup_c1(0, (nc.vector.tensor_copy,) * PACK)
         transpose_cand(0)
-        transpose_c1(0)
-        sup_codes = const.tile([P, N], U32, name="sup_codes", align_bytes=64)
-        sup_scales = const.tile([P, N], U8, name="sup_scales", align_bytes=64)
         quantise_c1_by_node(0)
-        quantise(sup_codes[:], sup_scales[:], sup_g[:])
-        regroup_c1(1, nc.scalar.copy, gpsimd_copy)
-
         w_g = const.tile([P, PARTS, H, PACK], BF16, name="w_g", align_bytes=64)
         nc.vector.tensor_copy(out=w_g[:], in_=w_sb[:].rearrange("q (g t) h -> q g h t", t=PACK))
+        sup_codes = const.tile([P, N], U32, name="sup_codes", align_bytes=64)
+        sup_scales = const.tile([P, N], U8, name="sup_scales", align_bytes=64)
+        quantise(sup_codes[:], sup_scales[:], sup_g[:])
+        hop_matmuls(0)
+
         bias_col = const.tile([P, 1], F32, name="bias_col")
         nc.vector.tensor_copy(out=bias_col[:], in_=bias_bf[:])
         w_codes = const.tile([P, PARTS, H], U32, name="w_codes", align_bytes=64)
         w_scales = const.tile([P, PARTS, H], U8, name="w_scales", align_bytes=64)
         for g in range(PARTS):
             quantise(w_codes[:, g, :], w_scales[:, g, :], w_g[:, g].rearrange("q h t -> q (h t)"))
+        regroup_c1(1, (nc.scalar.copy, nc.scalar.copy, nc.vector.tensor_copy, gpsimd_copy))
+        transpose_c1(0)
 
-        for k in range(B + 1):
+        last = B - 1
+        every_tile = range(NT)
+        for k in range(last):
             if k + AHEAD < B:
                 load(k + AHEAD)
-            if k < B:
-                hop_matmuls(k)
-                finish_c2(k)
-            if k + 1 < B:
-                transpose_cand(k + 1)
+            finish_c2(k, every_tile)
+            transpose_cand(k + 1)
             if k >= 1:
-                update_matmuls(k - 1)
-            if k + 1 < B:
-                transpose_c1(k + 1)
+                z = end_psum.tile([P, N], F32, name="z", tag="end")
+                update_matmuls(k - 1, z[:], range(PARTS), every_tile)
+                hc_t = squash(z[:], N)
+            transpose_c1(k + 1)
             if k >= 1:
-                transpose_back(k - 1)
+                bank = end_psum.tile([P, NT * H], F32, name="hc_minus_state", tag="end")
+                transpose_back(k - 1, hc_t, bank[:], every_tile)
             if k + 2 < B:
-                regroup_c1(k + 2, nc.scalar.copy, gpsimd_copy)
-            if k + 1 < B:
-                quantise_c1_by_node(k + 1)
-            if k < B:
-                quantise_cand_and_c1(k)
-                quantise_c2(k)
+                regroup_c1(k + 2, (nc.scalar.copy,) * (PACK - 1) + (gpsimd_copy,))
+            quantise_c1_by_node(k + 1)
+            quantise_cand_and_c1(k)
+            quantise_c2(k, every_tile)
             if k >= 1:
-                blend(k - 1)
+                blend(k - 1, bank[:], every_tile, nc.gpsimd.tensor_tensor)
+            hop_matmuls(k + 1)
+
+        shares = ((0, 1), (2,), (3,))
+        quantise_cand_and_c1(last)
+        finish_c2(last, shares[0])
+        z = tr_psum.tile([P, N], F32, name="z", tag="bank")
+        update_matmuls(last - 1, z[:], range(PARTS), every_tile)
+        hc_t = squash(z[:], N)
+        share_z = []
+        for tiles in shares[:2]:
+            share_z.append(tr_psum.tile([P, len(tiles) * P], F32, name="share_z", tag="bank"))
+            update_matmuls(last, share_z[-1][:], (0, 1), tiles)
+        bank = end_psum.tile([P, NT * H], F32, name="hc_minus_state", tag="end")
+        transpose_back(last - 1, hc_t, bank[:], every_tile)
+        share_z.append(tr_psum.tile([P, len(shares[2]) * P], F32, name="share_z", tag="bank"))
+        update_matmuls(last, share_z[-1][:], (0, 1), shares[2])
+        finish_c2(last, shares[1])
+        quantise_c2(last, shares[0])
+        blend(last - 1, bank[:], every_tile, nc.gpsimd.tensor_tensor)
+        finish_c2(last, shares[2])
+        share_bank = []
+
+        def end_update(n):
+            update_matmuls(last, share_z[n][:], (2,), shares[n])
+            return squash(share_z[n][:], len(shares[n]) * P)
+
+        def end_back(n, hc_t):
+            share_bank.append(hop_psum.tile([P, len(shares[n]) * H], F32, name="share_bank", tag="acc"))
+            transpose_back(last, hc_t, share_bank[-1][:], shares[n])
+
+        end_back(0, end_update(0))
+        quantise_c2(last, shares[1])
+        quantise_c2(last, shares[2])
+        hc_1 = end_update(1)
+        hc_2 = end_update(2)
+        end_back(1, hc_1)
+        end_back(2, hc_2)
+        for n in range(len(shares)):
+            blend(last, share_bank[n][:], shares[n], nc.vector.tensor_tensor)

@@ -79,10 +79,13 @@ def tile_agcrncell_pc_t_kernel(tc, supports, cand, c1, W_update, b_update, r, st
 
         def regroup_c1(b, copies):
             c1_by_node[b] = work.tile([P, GROUPED], BF16, name="c1_by_node", align_bytes=64)
-            dst = c1_by_node[b][:].rearrange("p (t q f j) -> p t q j f", t=PACK, f=4, j=PACK)
-            src = c1_sb[b][:].rearrange("p j (u q f e) -> p u e q j f", u=2, f=4, e=2)
+            dst = c1_by_node[b][:].rearrange("p (t q j) -> p t q j", t=PACK, j=PACK)
+            src = c1_sb[b][:].rearrange("p j (u q e) -> p u e q j", u=2, e=2)
             for t, copy in enumerate(copies):
-                copy(out=dst[:, t], in_=src[:, t // 2, t % 2])
+                to, of = dst[:, t], src[:, t // 2, t % 2]
+                if copy != gpsimd_copy:
+                    to, of = (x.rearrange("p (q f) j -> p q j f", f=4) for x in (to, of))
+                copy(out=to, in_=of)
 
         def transpose_cand(b):
             given_g[b] = work.tile([P, 2, GROUPED], BF16, name="given_g", align_bytes=64)
@@ -128,6 +131,20 @@ def tile_agcrncell_pc_t_kernel(tc, supports, cand, c1, W_update, b_update, r, st
                     op0=ALU.mult,
                     op1=ALU.subtract,
                 )
+
+        def finish_c2_tile_by_gpsimd(b, i):
+            c2_g[b] = work.tile([P, GROUPED], BF16, name="c2_g", align_bytes=64)
+            cols = slice(i * P * PACK, (i + 1) * P * PACK)
+            doubled = work.tile([P, P * PACK], F32, name="doubled")
+            nc.scalar.activation(
+                out=doubled[:].rearrange("q (w t) -> q w t", t=PACK),
+                in_=hop_acc[b][i][:].rearrange("q t w -> q w t"),
+                func=ACT.Copy,
+                scale=2.0,
+            )
+            nc.gpsimd.tensor_tensor(
+                out=c2_g[b][:, cols], in0=doubled[:], in1=given_g[b][:, 0, cols], op=ALU.subtract
+            )
 
         def quantise_cand_and_c1(b):
             xg_codes[b] = work.tile([P, PARTS * N], U32, name="xg_codes", align_bytes=64)
@@ -230,10 +247,14 @@ def tile_agcrncell_pc_t_kernel(tc, supports, cand, c1, W_update, b_update, r, st
 
         last = B - 1
         every_tile = range(NT)
+
+        def shared(b):
+            return b % 2 == 1 and b != last
+
         for k in range(last):
             if k + AHEAD < B:
                 load(k + AHEAD)
-            finish_c2(k, every_tile)
+            finish_c2(k, range(1, NT) if shared(k) else every_tile)
             transpose_cand(k + 1)
             if k >= 1:
                 z = end_psum.tile([P, N], F32, name="z", tag="end")
@@ -244,13 +265,16 @@ def tile_agcrncell_pc_t_kernel(tc, supports, cand, c1, W_update, b_update, r, st
                 bank = end_psum.tile([P, NT * H], F32, name="hc_minus_state", tag="end")
                 transpose_back(k - 1, hc_t, bank[:], every_tile)
             if k + 2 < B:
-                regroup_c1(k + 2, (nc.scalar.copy,) * (PACK - 1) + (gpsimd_copy,))
+                on_gpsimd = 0 if shared(k) else 2
+                regroup_c1(k + 2, (nc.scalar.copy,) * (PACK - on_gpsimd) + (gpsimd_copy,) * on_gpsimd)
             quantise_c1_by_node(k + 1)
             quantise_cand_and_c1(k)
             quantise_c2(k, every_tile)
+            hop_matmuls(k + 1)
+            if shared(k + 1):
+                finish_c2_tile_by_gpsimd(k + 1, 0)
             if k >= 1:
                 blend(k - 1, bank[:], every_tile, nc.gpsimd.tensor_tensor)
-            hop_matmuls(k + 1)
 
         shares = ((0, 1), (2,), (3,))
         quantise_cand_and_c1(last)

from contextlib import ExitStack

import concourse.mybir as mybir
from concourse.masks import make_identity

F32 = mybir.dt.float32
BF16 = mybir.dt.bfloat16
U32 = mybir.dt.uint32
U8 = mybir.dt.uint8
FP8X4 = mybir.dt.float8_e4m3fn_x4
ALU = mybir.AluOpType
ACT = mybir.ActivationFunctionType

P = 128
PACK = 4
B, N, C, H = 16, 512, 512, 128
PARTS = 3
NT = N // P
GROUPED = N * PACK
AHEAD = 4

FLOPS = 2 * B * N * N * C + 2 * B * N * PARTS * C * H


def tile_agcrncell_pc_t_kernel(tc, supports, cand, c1, W_update, b_update, r, state, out):
    nc = tc.nc
    with ExitStack() as stack:
        const = stack.enter_context(tc.tile_pool(name="const", bufs=1))
        big_in = stack.enter_context(tc.tile_pool(name="big_in", bufs=AHEAD + 1))
        gate_in = stack.enter_context(tc.tile_pool(name="gate_in", bufs=AHEAD + 3))
        work = stack.enter_context(tc.tile_pool(name="work", bufs=2))
        tr_psum = stack.enter_context(tc.psum_pool(name="tr_psum", bufs=3))
        hop_psum = stack.enter_context(tc.psum_pool(name="hop_psum", bufs=NT))
        end_psum = stack.enter_context(tc.psum_pool(name="end_psum", bufs=1))
        stack.enter_context(tc.manual_schedule())

        c1_sb, cand_sb, r_sb, state_sb = {}, {}, {}, {}
        c1_by_node, c1_codes, c1_scales = {}, {}, {}
        given_g, c2_g, xg_codes, xg_scales = {}, {}, {}, {}
        hop_acc = {}

        def load_c1(b):
            c1_sb[b] = big_in.tile([P, NT, C], BF16, name="c1_sb")
            nc.sync.dma_start(out=c1_sb[b][:], in_=c1[b].rearrange("(p i) c -> p i c", i=NT))

        def load_cand(b):
            cand_sb[b] = big_in.tile([P, NT, C], BF16, name="cand_sb")
            nc.sync.dma_start(out=cand_sb[b][:], in_=cand[b].rearrange("(p i) c -> p i c", i=NT))

        def load_gates(b):
            r_sb[b] = gate_in.tile([P, NT * H], BF16, name="r_sb")
            nc.sync.dma_start(out=r_sb[b][:], in_=r[b].rearrange("(p i) h -> p (i h)", i=NT))
            state_sb[b] = gate_in.tile([P, NT * H], BF16, name="state_sb")
            nc.sync.dma_start(out=state_sb[b][:], in_=state[b].rearrange("(p i) h -> p (i h)", i=NT))

        def load(b):
            load_c1(b)
            load_cand(b)
            load_gates(b)

        def transpose_words(word_block, grouped):
            grouped_words = grouped.bitcast(F32).rearrange("q (w u) -> q w u", u=2)
            for half in range(2):
                bank = tr_psum.tile([P, 2, 2 * P], F32, name="bank")
                for il in range(2):
                    for u in range(2):
                        nc.tensor.transpose(bank[:, u, il * P : (il + 1) * P], word_block(2 * half + il, u), ident[:])
                nc.scalar.copy(
                    out=grouped_words[:, half * 2 * P : (half + 1) * 2 * P, :],
                    in_=bank[:].rearrange("q u w -> q w u"),
                )

        def contiguous_words(x_sb):
            words = x_sb[:].bitcast(F32)
            return lambda i, u: words[:, i, u * P : (u + 1) * P]

        def gpsimd_copy(out, in_):
            nc.gpsimd.tensor_scalar(out=out, in0=in_, scalar1=1.0, scalar2=0.0, op0=ALU.mult, op1=ALU.add)

        def regroup_c1(b, copies):
            c1_by_node[b] = work.tile([P, GROUPED], BF16, name="c1_by_node", align_bytes=64)
            dst = c1_by_node[b][:].rearrange("p (t q j) -> p t q j", t=PACK, j=PACK)
            src = c1_sb[b][:].rearrange("p j (u q e) -> p u e q j", u=2, e=2)
            for t, copy in enumerate(copies):
                to, of = dst[:, t], src[:, t // 2, t % 2]
                if copy != gpsimd_copy:
                    to, of = (x.rearrange("p (q f) j -> p q j f", f=4) for x in (to, of))
                copy(out=to, in_=of)

        def transpose_cand(b):
            given_g[b] = work.tile([P, 2, GROUPED], BF16, name="given_g", align_bytes=64)
            transpose_words(contiguous_words(cand_sb[b]), given_g[b][:, 0, :])

        def transpose_c1(b):
            transpose_words(contiguous_words(c1_sb[b]), given_g[b][:, 1, :])

        def quantise(codes, scales, grouped):
            nc.vector.quantize_mx(out=codes.bitcast(FP8X4), scales=scales, in_=grouped)

        def quantise_c1_by_node(b):
            c1_codes[b] = work.tile([P, C], U32, name="c1_codes", align_bytes=64)
            c1_scales[b] = work.tile([P, C], U8, name="c1_scales", align_bytes=64)
            quantise(c1_codes[b][:], c1_scales[b][:], c1_by_node[b][:])

        def hop_matmuls(b):
            hop_acc[b] = []
            for i in range(NT):
                acc = hop_psum.tile([P, PACK, P], F32, name="acc")
                for t in range(PACK):
                    nc.tensor.matmul_mx(
                        out=acc[:, t, :],
                        lhsT=c1_codes[b][:, t * P : (t + 1) * P].bitcast(FP8X4),
                        lhsT_scale=c1_scales[b][:, t * P : (t + 1) * P],
                        rhs=sup_codes[:, i * P : (i + 1) * P].bitcast(FP8X4),
                        rhs_scale=sup_scales[:, i * P : (i + 1) * P],
                        start=True,
                        stop=True,
                    )
                hop_acc[b].append(acc)

        def finish_c2(b, tiles):
            if b not in c2_g:
                c2_g[b] = work.tile([P, GROUPED], BF16, name="c2_g", align_bytes=64)
            for i in tiles:
                cols = slice(i * P, (i + 1) * P)
                nc.vector.scalar_tensor_tensor(
                    out=c2_g[b][:].rearrange("q (w t) -> q w t", t=PACK)[:, cols, :],
                    in0=hop_acc[b][i][:].rearrange("q t w -> q w t"),
                    scalar=2.0,
                    in1=given_g[b][:, 0, :].rearrange("q (w t) -> q w t", t=PACK)[:, cols, :],
                    op0=ALU.mult,
                    op1=ALU.subtract,
                )

        def finish_c2_tile_by_gpsimd(b, i):
            c2_g[b] = work.tile([P, GROUPED], BF16, name="c2_g", align_bytes=64)
            cols = slice(i * P * PACK, (i + 1) * P * PACK)
            doubled = work.tile([P, P * PACK], F32, name="doubled")
            nc.scalar.activation(
                out=doubled[:].rearrange("q (w t) -> q w t", t=PACK),
                in_=hop_acc[b][i][:].rearrange("q t w -> q w t"),
                func=ACT.Copy,
                scale=2.0,
            )
            nc.gpsimd.tensor_tensor(
                out=c2_g[b][:, cols], in0=doubled[:], in1=given_g[b][:, 0, cols], op=ALU.subtract
            )

        def quantise_cand_and_c1(b):
            xg_codes[b] = work.tile([P, PARTS * N], U32, name="xg_codes", align_bytes=64)
            xg_scales[b] = work.tile([P, PARTS * N], U8, name="xg_scales", align_bytes=64)
            quantise(xg_codes[b][:, : 2 * N], xg_scales[b][:, : 2 * N], given_g[b][:].rearrange("q g x -> q (g x)"))

        def quantise_c2(b, tiles):
            words = slice(2 * N + tiles[0] * P, 2 * N + (tiles[-1] + 1) * P)
            grouped = c2_g[b][:, tiles[0] * P * PACK : (tiles[-1] + 1) * P * PACK]
            quantise(xg_codes[b][:, words], xg_scales[b][:, words], grouped)

        def update_matmuls(b, z, parts, tiles):
            for g in parts:
                words = slice(g * N + tiles[0] * P, g * N + (tiles[-1] + 1) * P)
                nc.tensor.matmul_mx(
                    out=z,
                    lhsT=w_codes[:, g, :].bitcast(FP8X4),
                    lhsT_scale=w_scales[:, g, :],
                    rhs=xg_codes[b][:, words].bitcast(FP8X4),
                    rhs_scale=xg_scales[b][:, words],
                    start=(g == 0),
                    stop=(g == PARTS - 1),
                )

        def squash(z, width):
            hc_t = work.tile([P, width], F32, name="hc_t")
            nc.scalar.activation(out=hc_t[:], in_=z, func=ACT.Tanh, bias=bias_col[:, 0:1], scale=1.0)
            return hc_t

        def transpose_back(b, hc_t, bank, tiles):
            for n, i in enumerate(tiles):
                nc.tensor.matmul(
                    out=bank[:, n * H : (n + 1) * H],
                    lhsT=hc_t[:, n * P : (n + 1) * P],
                    rhs=ident[:],
                    is_transpose=True,
                    start=(n == 0),
                    stop=False,
                )
            cols = slice(tiles[0] * H, (tiles[-1] + 1) * H)
            nc.tensor.matmul(out=bank, lhsT=minus_ident[:], rhs=state_sb[b][:, cols], start=False, stop=True)

        def blend(b, bank, tiles, subtract):
            cols = slice(tiles[0] * H, (tiles[-1] + 1) * H)
            width = len(tiles) * H
            step = work.tile([P, width], F32, name="step")
            nc.vector.scalar_tensor_tensor(
                out=step[:], in0=r_sb[b][:, cols], scalar=1.0, in1=bank, op0=ALU.subtract, op1=ALU.mult
            )
            result = work.tile([P, width], F32, name="result", bufs=6)
            subtract(out=result[:], in0=state_sb[b][:, cols], in1=step[:], op=ALU.subtract)
            rows = out[b].rearrange("(p i) h -> p (i h)", i=NT)
            nc.sync.dma_start(out=rows[:, cols], in_=result[:])

        load_c1(0)
        sup_sb = const.tile([P, NT, N], BF16, name="sup_sb")
        nc.sync.dma_start(out=sup_sb[:], in_=supports.rearrange("(p i) m -> p i m", i=NT))
        w_sb = const.tile([P, PARTS * PACK, H], BF16, name="w_sb")
        nc.sync.dma_start(
            out=w_sb[:].rearrange("q (a e) h -> q a e h", e=2),
            in_=W_update.rearrange("(a q e) h -> q a e h", q=P, e=2),
        )
        bias_bf = const.tile([P, 1], BF16, name="bias_bf")
        with nc.allow_non_contiguous_dma(reason="128 bias values, one to a partition"):
            nc.scalar.dma_start(out=bias_bf[:], in_=b_update.rearrange("(h o) -> h o", o=1))
        load_cand(0)
        load_c1(1)
        load_cand(1)
        load_gates(0)
        load_gates(1)
        for b in range(2, AHEAD):
            load(b)

        ident = const.tile([P, P], F32, name="ident")
        make_identity(nc, ident[:])
        minus_ident = const.tile([P, P], BF16, name="minus_ident")
        nc.vector.tensor_scalar_mul(out=minus_ident[:], in0=ident[:], scalar1=-1.0)

        sup_words = sup_sb[:].bitcast(F32).rearrange("p i (q s) -> p i q s", s=2)
        sup_g = const.tile([P, GROUPED], BF16, name="sup_g", align_bytes=64)
        transpose_words(lambda i, s: sup_words[:, i, :, s], sup_g[:])
        regroup_c1(0, (nc.vector.tensor_copy,) * PACK)
        transpose_cand(0)
        quantise_c1_by_node(0)
        w_g = const.tile([P, PARTS, H, PACK], BF16, name="w_g", align_bytes=64)
        nc.vector.tensor_copy(out=w_g[:], in_=w_sb[:].rearrange("q (g t) h -> q g h t", t=PACK))
        sup_codes = const.tile([P, N], U32, name="sup_codes", align_bytes=64)
        sup_scales = const.tile([P, N], U8, name="sup_scales", align_bytes=64)
        quantise(sup_codes[:], sup_scales[:], sup_g[:])
        hop_matmuls(0)

        bias_col = const.tile([P, 1], F32, name="bias_col")
        nc.vector.tensor_copy(out=bias_col[:], in_=bias_bf[:])
        w_codes = const.tile([P, PARTS, H], U32, name="w_codes", align_bytes=64)
        w_scales = const.tile([P, PARTS, H], U8, name="w_scales", align_bytes=64)
        for g in range(PARTS):
            quantise(w_codes[:, g, :], w_scales[:, g, :], w_g[:, g].rearrange("q h t -> q (h t)"))
        regroup_c1(1, (nc.scalar.copy, nc.scalar.copy, nc.vector.tensor_copy, gpsimd_copy))
        transpose_c1(0)

        last = B - 1
        every_tile = range(NT)

        def shared(b):
            return b % 2 == 1 and b != last

        for k in range(last):
            if k + AHEAD < B:
                load(k + AHEAD)
            finish_c2(k, range(1, NT) if shared(k) else every_tile)
            transpose_cand(k + 1)
            if k >= 1:
                z = end_psum.tile([P, N], F32, name="z", tag="end")
                update_matmuls(k - 1, z[:], range(PARTS), every_tile)
                hc_t = squash(z[:], N)
            transpose_c1(k + 1)
            if k >= 1:
                bank = end_psum.tile([P, NT * H], F32, name="hc_minus_state", tag="end")
                transpose_back(k - 1, hc_t, bank[:], every_tile)
            if k + 2 < B:
                on_gpsimd = 0 if shared(k) else 2
                regroup_c1(k + 2, (nc.scalar.copy,) * (PACK - on_gpsimd) + (gpsimd_copy,) * on_gpsimd)
            quantise_c1_by_node(k + 1)
            quantise_cand_and_c1(k)
            quantise_c2(k, every_tile)
            hop_matmuls(k + 1)
            if shared(k + 1):
                finish_c2_tile_by_gpsimd(k + 1, 0)
            if k >= 1:
                blend(k - 1, bank[:], every_tile, nc.gpsimd.tensor_tensor)

        shares = ((0, 1), (2,), (3,))
        quantise_cand_and_c1(last)
        finish_c2(last, shares[0])
        z = tr_psum.tile([P, N], F32, name="z", tag="bank")
        update_matmuls(last - 1, z[:], range(PARTS), every_tile)
        hc_t = squash(z[:], N)
        share_z = []
        for tiles in shares[:2]:
            share_z.append(tr_psum.tile([P, len(tiles) * P], F32, name="share_z", tag="bank"))
            update_matmuls(last, share_z[-1][:], (0, 1), tiles)
        bank = end_psum.tile([P, NT * H], F32, name="hc_minus_state", tag="end")
        transpose_back(last - 1, hc_t, bank[:], every_tile)
        share_z.append(tr_psum.tile([P, len(shares[2]) * P], F32, name="share_z", tag="bank"))
        update_matmuls(last, share_z[-1][:], (0, 1), shares[2])
        finish_c2(last, shares[1])
        quantise_c2(last, shares[0])
        blend(last - 1, bank[:], every_tile, nc.gpsimd.tensor_tensor)
        finish_c2(last, shares[2])
        share_bank = []

        def end_update(n):
            update_matmuls(last, share_z[n][:], (2,), shares[n])
            return squash(share_z[n][:], len(shares[n]) * P)

        def end_back(n, hc_t):
            share_bank.append(hop_psum.tile([P, len(shares[n]) * H], F32, name="share_bank", tag="acc"))
            transpose_back(last, hc_t, share_bank[-1][:], shares[n])

        end_back(0, end_update(0))
        quantise_c2(last, shares[1])
        quantise_c2(last, shares[2])
        hc_1 = end_update(1)
        hc_2 = end_update(2)
        end_back(1, hc_1)
        end_back(2, hc_2)
        for n in range(len(shares)):
            blend(last, share_bank[n][:], shares[n], nc.vector.tensor_tensor)
